import numpy as np
import ml_dtypes


def mxq(x, axis, fmt="e4m3"):
    dtype, down = {"e4m3": (ml_dtypes.float8_e4m3fn, 7), "e5m2": (ml_dtypes.float8_e5m2, 14)}[fmt]
    v = np.moveaxis(np.asarray(x, np.float32).astype(ml_dtypes.bfloat16).astype(np.float64), axis, -1)
    blocks = v.reshape(v.shape[:-1] + (-1, 32))
    amax = np.abs(blocks).max(-1, keepdims=True)
    byte = np.maximum(np.where(amax > 0, np.frexp(amax)[1] - 1 + 127, 0) - down, 1)
    scale = np.exp2(byte - 127.0)
    codes = (blocks / scale).astype(np.float32).astype(dtype).astype(np.float64)
    return np.moveaxis((codes * scale).reshape(v.shape), -1, axis)


WIDE = False


def mx_kscale(k):
    if not WIDE:
        return np.ones(k)
    levels = np.array([10, -10, 5, -5, 0])
    if k % 512:
        return np.exp2(np.random.permutation(np.resize(levels, k // 32))).repeat(32)
    a = np.empty((k // 512, 16))
    for p in range(k // 512):
        a[p, :8] = np.random.permutation(np.resize(levels, 8))
        for g in range(8):
            far = levels[np.abs(levels - a[p, g]) >= 10]
            a[p, g + 8] = far[np.random.randint(len(far))]
    return np.exp2(a.ravel()).repeat(32)


BF16 = ml_dtypes.bfloat16


def bf(x):
    return np.asarray(x, np.float32).astype(BF16)


def f64(x):
    return np.asarray(x).astype(np.float64)


B, L, D, H = 1, 1024, 512, 8


def setup_inputs():
    s = mx_kscale(D)
    return {"x": bf(np.random.standard_normal((B, L, D)) * s),
            "w": bf(np.random.standard_normal((H, D, D)) / np.sqrt(D) / s[:, None] * s[None, :])}


def reference(x, w):
    wq = mxq(f64(w), 1, "e4m3")
    xq = mxq(f64(x), 2, "e4m3")
    xs = (xq[None] @ wq[:, None]).reshape(H * B, L, D)
    return mxq(xs, 2, "e4m3") @ wq

@@ -1,0 +1,249 @@
+from contextlib import ExitStack
+
+import concourse.mybir as mybir
+from concourse.masks import make_identity
+
+H, L, D = 8, 1024, 512
+FLOPS = 2 * 2 * H * L * D * D
+
+F32 = mybir.dt.float32
+BF16 = mybir.dt.bfloat16
+U32 = mybir.dt.uint32
+U8 = mybir.dt.uint8
+FP8X4 = mybir.dt.float8_e4m3fn_x4
+
+P = 128
+PACK = 4
+LT = L // P
+BANK_DT = F32
+
+SKEW = 5
+QC = 2
+DQ = 1
+SCALAR_NUM, SCALAR_DEN = 27, 40
+W_COPY_AHEAD = 10
+W_QUANT_AHEAD = 4
+STORE_CHUNKS = 2
+LAST_STORES = {1: 0, 3: 2, 5: 4, 6: 6, 7: 7}
+
+
+def tile_multiheadattention_pa_kernel(tc, x, w, out):
+    nc = tc.nc
+    x_rows = x.flatten_outer_dims().rearrange("(p a) k -> p a k", a=LT)
+    w_rows = w.flatten_outer_dims()
+    out_rows = out.flatten_outer_dims()
+
+    with ExitStack() as ctx:
+        consts = ctx.enter_context(tc.tile_pool(name="consts", bufs=1))
+        w_pool = ctx.enter_context(tc.tile_pool(name="w_pool", bufs=H))
+        wg_pool = ctx.enter_context(tc.tile_pool(name="wg_pool", bufs=2))
+        xs_pool = ctx.enter_context(tc.tile_pool(name="xs_pool", bufs=3))
+        o_pool = ctx.enter_context(tc.tile_pool(name="o_pool", bufs=3))
+        psum = ctx.enter_context(tc.psum_pool(name="psum", bufs=4))
+
+        warm_in = consts.tile([P, 1], F32, name="warm_in")
+        warm_out = consts.tile([P, 1], F32, name="warm_out")
+        nc.vector.memset(warm_in[:], 0.0)
+        nc.scalar.copy(out=warm_out[:], in_=warm_in[:])
+
+        ident = consts.tile([P, P], F32, name="ident")
+        make_identity(nc, ident[:])
+
+        x_sb = consts.tile([P, LT, D], BF16, name="x_sb")
+        w_raw = []
+        for h in range(H):
+            w_raw_h = w_pool.tile([P, PACK, D], BF16, name="w_raw_h", tag="w_raw")
+            w_raw.append(w_raw_h)
+
+        def load_x(a0, a1):
+            nc.sync.dma_start(out=x_sb[:, a0:a1, :], in_=x_rows[:, a0:a1, :])
+
+        def load_w(h):
+            nc.sync.dma_start(
+                out=w_raw[h][:],
+                in_=w_rows[h * D : (h + 1) * D, :].rearrange("(p j) c -> p j c", j=PACK),
+            )
+
+        load_w(0)
+        load_x(0, 2)
+        load_x(2, 4)
+        load_x(4, 8)
+        for h in range(1, H):
+            load_w(h)
+
+        w_grouped = {}
+        w_codes = {}
+        w_scales = {}
+
+        def w_views(h, t0, t1):
+            dst = w_grouped[h][:, t0 * P * PACK : t1 * P * PACK].rearrange("p (t m j) -> p t m j", t=t1 - t0, j=PACK)
+            src = w_raw[h][:].rearrange("p j (m t) -> p t m j", t=PACK)[:, t0:t1, :, :]
+            return dst, src
+
+        def w_alloc(h):
+            wg = wg_pool.tile([P, D * PACK], BF16, name="wg", tag="wg", align_bytes=64)
+            w_grouped[h] = wg
+
+        def w_copy_first():
+            w_alloc(0)
+            dst, src = w_views(0, 0, 2)
+            nc.vector.tensor_copy(out=dst, in_=src)
+            dst, src = w_views(0, 3, 4)
+            nc.scalar.copy(out=dst, in_=src)
+            dst, src = w_views(0, 2, 3)
+            nc.vector.tensor_copy(out=dst, in_=src)
+
+        def w_copy(h, t):
+            if t == 0:
+                w_alloc(h)
+            dst, src = w_views(h, t, t + 1)
+            nc.vector.tensor_copy(out=dst, in_=src)
+
+        def w_quant(h):
+            wc = w_pool.tile([P, D], U32, name="wc", tag="w_codes", align_bytes=64)
+            ws = w_pool.tile([P, D], U8, name="ws", tag="w_scales", align_bytes=64)
+            nc.vector.quantize_mx(out=wc[:].bitcast(FP8X4), scales=ws[:], in_=w_grouped[h][:])
+            w_codes[h] = wc
+            w_scales[h] = ws
+
+        x_grouped = consts.tile([P, LT, P, PACK], BF16, name="x_grouped", align_bytes=64)
+        x_codes = consts.tile([P, L], U32, name="x_codes", align_bytes=64)
+        x_scales = consts.tile([P, L], U8, name="x_scales", align_bytes=64)
+
+        def x_transpose(pr):
+            xt = psum.tile([P, 2, 2, P], F32, name="xt", tag="s1")
+            for a2 in range(2):
+                words = x_sb[:, 2 * pr + a2, :].bitcast(F32)
+                for u in range(2):
+                    nc.tensor.transpose(xt[:, a2, u, :], words[:, u : D // 2 : 2], ident[:])
+            nc.scalar.copy(
+                out=x_grouped[:, 2 * pr : 2 * pr + 2, :, :].bitcast(F32),
+                in_=xt[:].rearrange("p a u r -> p a r u"),
+            )
+
+        def x_quant(pr):
+            cols = slice(2 * P * pr, 2 * P * (pr + 1))
+            nc.vector.quantize_mx(
+                out=x_codes[:, cols].bitcast(FP8X4),
+                scales=x_scales[:, cols],
+                in_=x_grouped[:, 2 * pr : 2 * pr + 2, :, :].rearrange("p a r j -> p (a r j)"),
+            )
+
+        xs_grouped = {}
+        xs_codes = {}
+        xs_scales = {}
+        o_sb = {}
+        banks = {}
+        accs = {}
+        reads = [0]
+
+        def psum_read(dst, src):
+            n = reads[0]
+            reads[0] = n + 1
+            if ((n + 1) * SCALAR_NUM) // SCALAR_DEN != (n * SCALAR_NUM) // SCALAR_DEN:
+                nc.scalar.copy(out=dst, in_=src)
+            else:
+                nc.vector.tensor_copy(out=dst, in_=src)
+
+        def stage1(h, i):
+            if i == 0:
+                xg = xs_pool.tile([P, L, PACK], BF16, name="xg", tag="xs_grouped", align_bytes=64)
+                xc = xs_pool.tile([P, L], U32, name="xc", tag="xs_codes", align_bytes=64)
+                xsc = xs_pool.tile([P, L], U8, name="xsc", tag="xs_scales", align_bytes=64)
+                xs_grouped[h] = xg
+                xs_codes[h] = xc
+                xs_scales[h] = xsc
+            bank = psum.tile([P, PACK, P], BANK_DT, name="bank", tag="s1")
+            cols = slice(i * P, (i + 1) * P)
+            for t in range(PACK):
+                chans = slice(t * P, (t + 1) * P)
+                nc.tensor.matmul_mx(
+                    out=bank[:, t, :],
+                    lhsT=w_codes[h][:, chans].bitcast(FP8X4),
+                    lhsT_scale=w_scales[h][:, chans],
+                    rhs=x_codes[:, cols].bitcast(FP8X4),
+                    rhs_scale=x_scales[:, cols],
+                    start=True,
+                    stop=True,
+                )
+            banks[(h, i)] = bank
+
+        def read_bank(h, i):
+            psum_read(xs_grouped[h][:, i * P : (i + 1) * P, :], banks[(h, i)][:].rearrange("p t l -> p l t"))
+
+        def xs_quant(h, k):
+            cols = slice(k * QC * P, (k + 1) * QC * P)
+            nc.vector.quantize_mx(
+                out=xs_codes[h][:, cols].bitcast(FP8X4),
+                scales=xs_scales[h][:, cols],
+                in_=xs_grouped[h][:, cols, :].rearrange("p l j -> p (l j)"),
+            )
+
+        def stage2(h, i):
+            if i == 0:
+                ot = o_pool.tile([P, LT, D], F32, name="ot", tag="o_sb")
+                o_sb[h] = ot
+            acc = psum.tile([P, D], F32, name="acc", tag="s2")
+            cols = slice(i * P, (i + 1) * P)
+            nc.tensor.matmul_mx(
+                out=acc[:],
+                lhsT=xs_codes[h][:, cols].bitcast(FP8X4),
+                lhsT_scale=xs_scales[h][:, cols],
+                rhs=w_codes[h][:].bitcast(FP8X4),
+                rhs_scale=w_scales[h][:],
+                start=True,
+                stop=True,
+            )
+            accs[(h, i)] = acc
+
+        def read_acc(h, i):
+            psum_read(
+                o_sb[h][:, i, :].rearrange("p (m t) -> p m t", t=PACK),
+                accs[(h, i)][:].rearrange("p (t m) -> p m t", t=PACK),
+            )
+
+        def store(h, a0, a1):
+            nc.sync.dma_start(
+                out=out_rows[h * L : (h + 1) * L, :].rearrange("(p a) e -> p a e", a=LT)[:, a0:a1, :],
+                in_=o_sb[h][:, a0:a1, :],
+            )
+
+        with tc.manual_schedule():
+            w_copy_first()
+            x_transpose(0)
+            w_quant(0)
+            x_quant(0)
+            x_transpose(1)
+            x_quant(1)
+
+            for g in range(H * LT + SKEW):
+                g2 = g - SKEW
+                if g < H * LT:
+                    stage1(g // LT, g % LT)
+                if g2 >= 0:
+                    stage2(g2 // LT, g2 % LT)
+                if g == 0:
+                    x_transpose(2)
+                    x_transpose(3)
+                if g < H * LT:
+                    read_bank(g // LT, g % LT)
+                if g2 >= 0:
+                    read_acc(g2 // LT, g2 % LT)
+                if g in (1, 2):
+                    x_quant(g + 1)
+                gq = g - DQ
+                if 0 <= gq < H * LT and gq % QC == QC - 1:
+                    xs_quant(gq // LT, (gq % LT) // QC)
+                for h in range(1, H):
+                    for t in range(PACK):
+                        if g == max(t, LT * h - W_COPY_AHEAD + t):
+                            w_copy(h, t)
+                    if g == max(5, LT * h - W_QUANT_AHEAD):
+                        w_quant(h)
+                if g2 >= 0:
+                    h2, i2 = g2 // LT, g2 % LT
+                    if h2 < H - 1:
+                        if i2 % STORE_CHUNKS == STORE_CHUNKS - 1:
+                            store(h2, i2 + 1 - STORE_CHUNKS, i2 + 1)
+                    elif i2 in LAST_STORES:
+                        store(h2, LAST_STORES[i2], i2 + 1)

@@ -17,11 +17,12 @@ PACK = 4
 LT = L // P
 BANK_DT = F32
 
-SKEW = 5
-QC = 2
+SKEW = 7
+QC = 4
 DQ = 1
 SCALAR_NUM, SCALAR_DEN = 27, 40
 W_COPY_AHEAD = 10
+W_SLICES = 4
 W_QUANT_AHEAD = 4
 STORE_CHUNKS = 2
 LAST_STORES = {1: 0, 3: 2, 5: 4, 6: 6, 7: 7}
@@ -76,8 +77,8 @@ def tile_multiheadattention_pa_kernel(tc, x, w, out):
         w_scales = {}
 
         def w_views(h, t0, t1):
-            dst = w_grouped[h][:, t0 * P * PACK : t1 * P * PACK].rearrange("p (t m j) -> p t m j", t=t1 - t0, j=PACK)
-            src = w_raw[h][:].rearrange("p j (m t) -> p t m j", t=PACK)[:, t0:t1, :, :]
+            dst = w_grouped[h][:, t0 * P * PACK : t1 * P * PACK].rearrange("p (t m j) -> p m j t", t=t1 - t0, j=PACK)
+            src = w_raw[h][:].rearrange("p j (m t) -> p m j t", t=PACK)[:, :, :, t0:t1]
             return dst, src
 
         def w_alloc(h):
@@ -96,7 +97,7 @@ def tile_multiheadattention_pa_kernel(tc, x, w, out):
         def w_copy(h, t):
             if t == 0:
                 w_alloc(h)
-            dst, src = w_views(h, t, t + 1)
+            dst, src = w_views(h, t, t + W_SLICES)
             nc.vector.tensor_copy(out=dst, in_=src)
 
         def w_quant(h):
@@ -121,12 +122,12 @@ def tile_multiheadattention_pa_kernel(tc, x, w, out):
                 in_=xt[:].rearrange("p a u r -> p a r u"),
             )
 
-        def x_quant(pr):
-            cols = slice(2 * P * pr, 2 * P * (pr + 1))
+        def x_quant(a0, a1):
+            cols = slice(P * a0, P * a1)
             nc.vector.quantize_mx(
                 out=x_codes[:, cols].bitcast(FP8X4),
                 scales=x_scales[:, cols],
-                in_=x_grouped[:, 2 * pr : 2 * pr + 2, :, :].rearrange("p a r j -> p (a r j)"),
+                in_=x_grouped[:, a0:a1, :, :].rearrange("p a r j -> p (a r j)"),
             )
 
         xs_grouped = {}
@@ -212,9 +213,9 @@ def tile_multiheadattention_pa_kernel(tc, x, w, out):
             w_copy_first()
             x_transpose(0)
             w_quant(0)
-            x_quant(0)
+            x_quant(0, 2)
             x_transpose(1)
-            x_quant(1)
+            x_quant(2, 4)
 
             for g in range(H * LT + SKEW):
                 g2 = g - SKEW
@@ -229,13 +230,13 @@ def tile_multiheadattention_pa_kernel(tc, x, w, out):
                     read_bank(g // LT, g % LT)
                 if g2 >= 0:
                     read_acc(g2 // LT, g2 % LT)
-                if g in (1, 2):
-                    x_quant(g + 1)
+                if g == 1:
+                    x_quant(4, 8)
                 gq = g - DQ
                 if 0 <= gq < H * LT and gq % QC == QC - 1:
                     xs_quant(gq // LT, (gq % LT) // QC)
                 for h in range(1, H):
-                    for t in range(PACK):
+                    for t in range(0, PACK, W_SLICES):
                         if g == max(t, LT * h - W_COPY_AHEAD + t):
                             w_copy(h, t)
                     if g == max(5, LT * h - W_QUANT_AHEAD):

@@ -20,7 +20,8 @@ BANK_DT = F32
 SKEW = 7
 QC = 4
 DQ = 1
-SCALAR_NUM, SCALAR_DEN = 27, 40
+SCALAR_NUM, SCALAR_DEN = 11, 16
+TAIL_FROM = 112
 W_COPY_AHEAD = 10
 W_SLICES = 4
 W_QUANT_AHEAD = 4
@@ -141,7 +142,11 @@ def tile_multiheadattention_pa_kernel(tc, x, w, out):
         def psum_read(dst, src):
             n = reads[0]
             reads[0] = n + 1
-            if ((n + 1) * SCALAR_NUM) // SCALAR_DEN != (n * SCALAR_NUM) // SCALAR_DEN:
+            if n < TAIL_FROM:
+                on_scalar = ((n + 1) * SCALAR_NUM) // SCALAR_DEN != (n * SCALAR_NUM) // SCALAR_DEN
+            else:
+                on_scalar = (n - TAIL_FROM) % 2 == 1
+            if on_scalar:
                 nc.scalar.copy(out=dst, in_=src)
             else:
                 nc.vector.tensor_copy(out=dst, in_=src)

from contextlib import ExitStack

import concourse.mybir as mybir
from concourse.masks import make_identity

H, L, D = 8, 1024, 512
FLOPS = 2 * 2 * H * L * D * D

F32 = mybir.dt.float32
BF16 = mybir.dt.bfloat16
U32 = mybir.dt.uint32
U8 = mybir.dt.uint8
FP8X4 = mybir.dt.float8_e4m3fn_x4

P = 128
PACK = 4
LT = L // P
BANK_DT = F32

SKEW = 7
QC = 4
DQ = 1
SCALAR_NUM, SCALAR_DEN = 11, 16
TAIL_FROM = 112
W_COPY_AHEAD = 10
W_SLICES = 4
W_QUANT_AHEAD = 4
STORE_CHUNKS = 2
LAST_STORES = {1: 0, 3: 2, 5: 4, 6: 6, 7: 7}


def tile_multiheadattention_pa_kernel(tc, x, w, out):
    nc = tc.nc
    x_rows = x.flatten_outer_dims().rearrange("(p a) k -> p a k", a=LT)
    w_rows = w.flatten_outer_dims()
    out_rows = out.flatten_outer_dims()

    with ExitStack() as ctx:
        consts = ctx.enter_context(tc.tile_pool(name="consts", bufs=1))
        w_pool = ctx.enter_context(tc.tile_pool(name="w_pool", bufs=H))
        wg_pool = ctx.enter_context(tc.tile_pool(name="wg_pool", bufs=2))
        xs_pool = ctx.enter_context(tc.tile_pool(name="xs_pool", bufs=3))
        o_pool = ctx.enter_context(tc.tile_pool(name="o_pool", bufs=3))
        psum = ctx.enter_context(tc.psum_pool(name="psum", bufs=4))

        warm_in = consts.tile([P, 1], F32, name="warm_in")
        warm_out = consts.tile([P, 1], F32, name="warm_out")
        nc.vector.memset(warm_in[:], 0.0)
        nc.scalar.copy(out=warm_out[:], in_=warm_in[:])

        ident = consts.tile([P, P], F32, name="ident")
        make_identity(nc, ident[:])

        x_sb = consts.tile([P, LT, D], BF16, name="x_sb")
        w_raw = []
        for h in range(H):
            w_raw_h = w_pool.tile([P, PACK, D], BF16, name="w_raw_h", tag="w_raw")
            w_raw.append(w_raw_h)

        def load_x(a0, a1):
            nc.sync.dma_start(out=x_sb[:, a0:a1, :], in_=x_rows[:, a0:a1, :])

        def load_w(h):
            nc.sync.dma_start(
                out=w_raw[h][:],
                in_=w_rows[h * D : (h + 1) * D, :].rearrange("(p j) c -> p j c", j=PACK),
            )

        load_w(0)
        load_x(0, 2)
        load_x(2, 4)
        load_x(4, 8)
        for h in range(1, H):
            load_w(h)

        w_grouped = {}
        w_codes = {}
        w_scales = {}

        def w_views(h, t0, t1):
            dst = w_grouped[h][:, t0 * P * PACK : t1 * P * PACK].rearrange("p (t m j) -> p m j t", t=t1 - t0, j=PACK)
            src = w_raw[h][:].rearrange("p j (m t) -> p m j t", t=PACK)[:, :, :, t0:t1]
            return dst, src

        def w_alloc(h):
            wg = wg_pool.tile([P, D * PACK], BF16, name="wg", tag="wg", align_bytes=64)
            w_grouped[h] = wg

        def w_copy_first():
            w_alloc(0)
            dst, src = w_views(0, 0, 2)
            nc.vector.tensor_copy(out=dst, in_=src)
            dst, src = w_views(0, 3, 4)
            nc.scalar.copy(out=dst, in_=src)
            dst, src = w_views(0, 2, 3)
            nc.vector.tensor_copy(out=dst, in_=src)

        def w_copy(h, t):
            if t == 0:
                w_alloc(h)
            dst, src = w_views(h, t, t + W_SLICES)
            nc.vector.tensor_copy(out=dst, in_=src)

        def w_quant(h):
            wc = w_pool.tile([P, D], U32, name="wc", tag="w_codes", align_bytes=64)
            ws = w_pool.tile([P, D], U8, name="ws", tag="w_scales", align_bytes=64)
            nc.vector.quantize_mx(out=wc[:].bitcast(FP8X4), scales=ws[:], in_=w_grouped[h][:])
            w_codes[h] = wc
            w_scales[h] = ws

        x_grouped = consts.tile([P, LT, P, PACK], BF16, name="x_grouped", align_bytes=64)
        x_codes = consts.tile([P, L], U32, name="x_codes", align_bytes=64)
        x_scales = consts.tile([P, L], U8, name="x_scales", align_bytes=64)

        def x_transpose(pr):
            xt = psum.tile([P, 2, 2, P], F32, name="xt", tag="s1")
            for a2 in range(2):
                words = x_sb[:, 2 * pr + a2, :].bitcast(F32)
                for u in range(2):
                    nc.tensor.transpose(xt[:, a2, u, :], words[:, u : D // 2 : 2], ident[:])
            nc.scalar.copy(
                out=x_grouped[:, 2 * pr : 2 * pr + 2, :, :].bitcast(F32),
                in_=xt[:].rearrange("p a u r -> p a r u"),
            )

        def x_quant(a0, a1):
            cols = slice(P * a0, P * a1)
            nc.vector.quantize_mx(
                out=x_codes[:, cols].bitcast(FP8X4),
                scales=x_scales[:, cols],
                in_=x_grouped[:, a0:a1, :, :].rearrange("p a r j -> p (a r j)"),
            )

        xs_grouped = {}
        xs_codes = {}
        xs_scales = {}
        o_sb = {}
        banks = {}
        accs = {}
        reads = [0]

        def psum_read(dst, src):
            n = reads[0]
            reads[0] = n + 1
            if n < TAIL_FROM:
                on_scalar = ((n + 1) * SCALAR_NUM) // SCALAR_DEN != (n * SCALAR_NUM) // SCALAR_DEN
            else:
                on_scalar = (n - TAIL_FROM) % 2 == 1
            if on_scalar:
                nc.scalar.copy(out=dst, in_=src)
            else:
                nc.vector.tensor_copy(out=dst, in_=src)

        def stage1(h, i):
            if i == 0:
                xg = xs_pool.tile([P, L, PACK], BF16, name="xg", tag="xs_grouped", align_bytes=64)
                xc = xs_pool.tile([P, L], U32, name="xc", tag="xs_codes", align_bytes=64)
                xsc = xs_pool.tile([P, L], U8, name="xsc", tag="xs_scales", align_bytes=64)
                xs_grouped[h] = xg
                xs_codes[h] = xc
                xs_scales[h] = xsc
            bank = psum.tile([P, PACK, P], BANK_DT, name="bank", tag="s1")
            cols = slice(i * P, (i + 1) * P)
            for t in range(PACK):
                chans = slice(t * P, (t + 1) * P)
                nc.tensor.matmul_mx(
                    out=bank[:, t, :],
                    lhsT=w_codes[h][:, chans].bitcast(FP8X4),
                    lhsT_scale=w_scales[h][:, chans],
                    rhs=x_codes[:, cols].bitcast(FP8X4),
                    rhs_scale=x_scales[:, cols],
                    start=True,
                    stop=True,
                )
            banks[(h, i)] = bank

        def read_bank(h, i):
            psum_read(xs_grouped[h][:, i * P : (i + 1) * P, :], banks[(h, i)][:].rearrange("p t l -> p l t"))

        def xs_quant(h, k):
            cols = slice(k * QC * P, (k + 1) * QC * P)
            nc.vector.quantize_mx(
                out=xs_codes[h][:, cols].bitcast(FP8X4),
                scales=xs_scales[h][:, cols],
                in_=xs_grouped[h][:, cols, :].rearrange("p l j -> p (l j)"),
            )

        def stage2(h, i):
            if i == 0:
                ot = o_pool.tile([P, LT, D], F32, name="ot", tag="o_sb")
                o_sb[h] = ot
            acc = psum.tile([P, D], F32, name="acc", tag="s2")
            cols = slice(i * P, (i + 1) * P)
            nc.tensor.matmul_mx(
                out=acc[:],
                lhsT=xs_codes[h][:, cols].bitcast(FP8X4),
                lhsT_scale=xs_scales[h][:, cols],
                rhs=w_codes[h][:].bitcast(FP8X4),
                rhs_scale=w_scales[h][:],
                start=True,
                stop=True,
            )
            accs[(h, i)] = acc

        def read_acc(h, i):
            psum_read(
                o_sb[h][:, i, :].rearrange("p (m t) -> p m t", t=PACK),
                accs[(h, i)][:].rearrange("p (t m) -> p m t", t=PACK),
            )

        def store(h, a0, a1):
            nc.sync.dma_start(
                out=out_rows[h * L : (h + 1) * L, :].rearrange("(p a) e -> p a e", a=LT)[:, a0:a1, :],
                in_=o_sb[h][:, a0:a1, :],
            )

        with tc.manual_schedule():
            w_copy_first()
            x_transpose(0)
            w_quant(0)
            x_quant(0, 2)
            x_transpose(1)
            x_quant(2, 4)

            for g in range(H * LT + SKEW):
                g2 = g - SKEW
                if g < H * LT:
                    stage1(g // LT, g % LT)
                if g2 >= 0:
                    stage2(g2 // LT, g2 % LT)
                if g == 0:
                    x_transpose(2)
                    x_transpose(3)
                if g < H * LT:
                    read_bank(g // LT, g % LT)
                if g2 >= 0:
                    read_acc(g2 // LT, g2 % LT)
                if g == 1:
                    x_quant(4, 8)
                gq = g - DQ
                if 0 <= gq < H * LT and gq % QC == QC - 1:
                    xs_quant(gq // LT, (gq % LT) // QC)
                for h in range(1, H):
                    for t in range(0, PACK, W_SLICES):
                        if g == max(t, LT * h - W_COPY_AHEAD + t):
                            w_copy(h, t)
                    if g == max(5, LT * h - W_QUANT_AHEAD):
                        w_quant(h)
                if g2 >= 0:
                    h2, i2 = g2 // LT, g2 % LT
                    if h2 < H - 1:
                        if i2 % STORE_CHUNKS == STORE_CHUNKS - 1:
                            store(h2, i2 + 1 - STORE_CHUNKS, i2 + 1)
                    elif i2 in LAST_STORES:
                        store(h2, LAST_STORES[i2], i2 + 1)
